import numpy as np
import ml_dtypes


def mxq(x, axis, fmt="e4m3"):
    dtype, down = {"e4m3": (ml_dtypes.float8_e4m3fn, 7), "e5m2": (ml_dtypes.float8_e5m2, 14)}[fmt]
    v = np.moveaxis(np.asarray(x, np.float32).astype(ml_dtypes.bfloat16).astype(np.float64), axis, -1)
    blocks = v.reshape(v.shape[:-1] + (-1, 32))
    amax = np.abs(blocks).max(-1, keepdims=True)
    byte = np.maximum(np.where(amax > 0, np.frexp(amax)[1] - 1 + 127, 0) - down, 1)
    scale = np.exp2(byte - 127.0)
    codes = (blocks / scale).astype(np.float32).astype(dtype).astype(np.float64)
    return np.moveaxis((codes * scale).reshape(v.shape), -1, axis)


WIDE = False


def mx_kscale(k):
    if not WIDE:
        return np.ones(k)
    levels = np.array([10, -10, 5, -5, 0])
    if k % 512:
        return np.exp2(np.random.permutation(np.resize(levels, k // 32))).repeat(32)
    a = np.empty((k // 512, 16))
    for p in range(k // 512):
        a[p, :8] = np.random.permutation(np.resize(levels, 8))
        for g in range(8):
            far = levels[np.abs(levels - a[p, g]) >= 10]
            a[p, g + 8] = far[np.random.randint(len(far))]
    return np.exp2(a.ravel()).repeat(32)


BF16 = ml_dtypes.bfloat16


def bf(x):
    return np.asarray(x, np.float32).astype(BF16)


def f64(x):
    return np.asarray(x).astype(np.float64)


B, N, DIM, HEADS, DIM_HEAD = 2, 64, 512, 16, 64
INNER = HEADS * DIM_HEAD


def setup_inputs():
    s = mx_kscale(DIM)
    return {"x": bf(np.random.standard_normal((B, N, DIM)) * s),
            "W": bf(np.random.standard_normal((3 * INNER, DIM)) / np.sqrt(DIM) / s[None, :])}


def reference(x, W):
    b, n, _ = x.shape
    qkv = mxq(f64(x), 2, "e4m3") @ mxq(f64(W), 1, "e4m3").T
    q, k, v = np.split(qkv, 3, axis=-1)

    def to_heads(t):
        return t.reshape(b, n, HEADS, DIM_HEAD).transpose(0, 2, 1, 3)

    return to_heads(q), to_heads(k), to_heads(v)

@@ -1,0 +1,144 @@
+from contextlib import ExitStack
+
+import concourse.mybir as mybir
+from concourse.masks import make_identity
+
+BF16 = mybir.dt.bfloat16
+F32 = mybir.dt.float32
+U32 = mybir.dt.uint32
+U8 = mybir.dt.uint8
+FP8X4 = mybir.dt.float8_e4m3fn_x4
+
+P = 128
+PACK = 4
+BATCH, TOKENS, DIM = 2, 64, 512
+HEADS, DIM_HEAD = 16, 64
+PARTS = 3
+WORDS = DIM // 2
+HALVES = WORDS // P
+CHUNK = 512
+ROWS = CHUNK // P
+CHUNKS = PARTS * HEADS * DIM_HEAD // CHUNK
+CHUNKS_PER_PART = HEADS * DIM_HEAD // CHUNK
+CHUNK_HEADS = CHUNK // DIM_HEAD
+BANK_ROWS = 2
+
+QUANTISE_LAG, MULTIPLY_LAG, STORE_LAG = 1, 2, 3
+
+FLOPS = 2 * BATCH * TOKENS * DIM * PARTS * HEADS * DIM_HEAD
+
+
+def tile_get_qkv_s_kernel(tc, x, W, out_0, out_1, out_2):
+    nc = tc.nc
+    outs = [out_0, out_1, out_2]
+
+    with ExitStack() as ctx:
+        keep = ctx.enter_context(tc.tile_pool(name="keep", bufs=1))
+        stage = ctx.enter_context(tc.tile_pool(name="stage", bufs=3))
+        psum_x = ctx.enter_context(tc.psum_pool(name="psum_x", bufs=1))
+        psum_w = ctx.enter_context(tc.psum_pool(name="psum_w", bufs=4))
+        psum_acc = ctx.enter_context(tc.psum_pool(name="psum_acc", bufs=3))
+        ctx.enter_context(tc.manual_schedule())
+
+        x_raw = keep.tile([P, DIM], BF16)
+        for b in range(BATCH):
+            nc.sync.dma_start(out=x_raw[b:P:BATCH, :], in_=x[b, :, :])
+        w_raw = []
+        for c in range(CHUNKS):
+            raw = keep.tile([P, ROWS * DIM], BF16, name="w_raw%d" % c)
+            nc.sync.dma_start(
+                out=raw[:],
+                in_=W[c * CHUNK : (c + 1) * CHUNK, :].rearrange("(p r) d -> p (r d)", r=ROWS),
+            )
+            w_raw.append(raw)
+
+        ident = keep.tile([P, P], F32)
+        make_identity(nc, ident[:])
+
+        x_codes = keep.tile([P, P], U32, align_bytes=64)
+        x_scales = keep.tile([P, P], U8, align_bytes=64)
+        w_codes = keep.tile([P, CHUNKS, CHUNK], U32, align_bytes=64)
+        w_scales = keep.tile([P, CHUNKS, CHUNK], U8, align_bytes=64)
+
+        def multiply_chunk(c):
+            acc = psum_acc.tile([P, CHUNK], F32)
+            nc.tensor.matmul_mx(
+                out=acc[:],
+                lhsT=x_codes[:].bitcast(FP8X4),
+                lhsT_scale=x_scales[:],
+                rhs=w_codes[:, c, :].bitcast(FP8X4),
+                rhs_scale=w_scales[:, c, :],
+                start=True,
+                stop=True,
+            )
+            return acc
+
+        def transpose_x():
+            x_words = x_raw[:].bitcast(F32)
+            turned = psum_x.tile([P, HALVES, P], F32)
+            for half in range(HALVES):
+                nc.tensor.transpose(turned[:, half, :], x_words[:, half:WORDS:HALVES], ident[:])
+            grouped = stage.tile([P, P * PACK], BF16, name="x_grouped", align_bytes=64)
+            nc.scalar.copy(
+                out=grouped[:].bitcast(F32).rearrange("q (m h) -> q m h", h=HALVES),
+                in_=turned[:].rearrange("q h m -> q m h"),
+            )
+            return grouped
+
+        def transpose_chunk(c):
+            w_words = w_raw[c][:].bitcast(F32)
+            grouped = stage.tile([P, CHUNK * PACK], BF16, name="w_grouped", align_bytes=64)
+            grouped_words = grouped[:].bitcast(F32)
+            bank_words = BANK_ROWS * P * HALVES
+            for bank in range(ROWS // BANK_ROWS):
+                turned = psum_w.tile([P, BANK_ROWS, HALVES, P], F32)
+                for r in range(BANK_ROWS):
+                    for half in range(HALVES):
+                        first = (bank * BANK_ROWS + r) * WORDS
+                        nc.tensor.transpose(
+                            turned[:, r, half, :], w_words[:, first + half : first + WORDS : HALVES], ident[:]
+                        )
+                nc.scalar.copy(
+                    out=grouped_words[:, bank * bank_words : (bank + 1) * bank_words].rearrange(
+                        "q (r p h) -> q r p h", r=BANK_ROWS, h=HALVES
+                    ),
+                    in_=turned[:].rearrange("q r h p -> q r p h"),
+                )
+            return grouped
+
+        def store_chunk(c, acc):
+            result = keep.tile([P, CHUNK], F32, name="result%d" % c)
+            nc.vector.tensor_copy(
+                out=result[:].rearrange("m (p r) -> m p r", r=ROWS),
+                in_=acc[:].rearrange("m (r p) -> m p r", r=ROWS),
+            )
+            part = outs[c // CHUNKS_PER_PART]
+            head = (c % CHUNKS_PER_PART) * CHUNK_HEADS
+            for b in range(BATCH):
+                nc.sync.dma_start(
+                    out=part[b, head : head + CHUNK_HEADS, :, :].rearrange("h n d -> n h d"),
+                    in_=result[b:P:BATCH, :].rearrange("n (h d) -> n h d", d=DIM_HEAD),
+                )
+
+        x_grouped = transpose_x()
+        nc.vector.quantize_mx(out=x_codes[:].bitcast(FP8X4), scales=x_scales[:], in_=x_grouped[:])
+
+        grouped = {}
+        acc = {}
+        for step in range(CHUNKS + STORE_LAG):
+            if step < CHUNKS:
+                grouped[step] = transpose_chunk(step)
+
+            c = step - STORE_LAG
+            if c >= 0:
+                store_chunk(c, acc[c])
+
+            c = step - QUANTISE_LAG
+            if 0 <= c < CHUNKS:
+                nc.vector.quantize_mx(
+                    out=w_codes[:, c, :].bitcast(FP8X4), scales=w_scales[:, c, :], in_=grouped[c][:]
+                )
+
+            c = step - MULTIPLY_LAG
+            if 0 <= c < CHUNKS:
+                acc[c] = multiply_chunk(c)

@@ -16,16 +16,17 @@ HEADS, DIM_HEAD = 16, 64
 PARTS = 3
 WORDS = DIM // 2
 HALVES = WORDS // P
-CHUNK = 512
-ROWS = CHUNK // P
-CHUNKS = PARTS * HEADS * DIM_HEAD // CHUNK
-CHUNKS_PER_PART = HEADS * DIM_HEAD // CHUNK
-CHUNK_HEADS = CHUNK // DIM_HEAD
 BANK_ROWS = 2
+PART_ROWS = HEADS * DIM_HEAD
+CHUNK = 512
+CHUNKS = PARTS * PART_ROWS // CHUNK
+BANK = BANK_ROWS * P
+BANKS = CHUNK // BANK
 
-QUANTISE_LAG, MULTIPLY_LAG, STORE_LAG = 1, 2, 3
+PIECES = [2, 1, 1, 1, 1, 2]
+LAST = CHUNKS - 1
 
-FLOPS = 2 * BATCH * TOKENS * DIM * PARTS * HEADS * DIM_HEAD
+FLOPS = 2 * BATCH * TOKENS * DIM * PARTS * PART_ROWS
 
 
 def tile_get_qkv_s_kernel(tc, x, W, out_0, out_1, out_2):
@@ -35,23 +36,27 @@ def tile_get_qkv_s_kernel(tc, x, W, out_0, out_1, out_2):
     with ExitStack() as ctx:
         keep = ctx.enter_context(tc.tile_pool(name="keep", bufs=1))
         stage = ctx.enter_context(tc.tile_pool(name="stage", bufs=3))
-        psum_x = ctx.enter_context(tc.psum_pool(name="psum_x", bufs=1))
         psum_w = ctx.enter_context(tc.psum_pool(name="psum_w", bufs=4))
-        psum_acc = ctx.enter_context(tc.psum_pool(name="psum_acc", bufs=3))
+        psum_acc = ctx.enter_context(tc.psum_pool(name="psum_acc", bufs=4))
         ctx.enter_context(tc.manual_schedule())
 
         x_raw = keep.tile([P, DIM], BF16)
-        for b in range(BATCH):
-            nc.sync.dma_start(out=x_raw[b:P:BATCH, :], in_=x[b, :, :])
         w_raw = []
         for c in range(CHUNKS):
-            raw = keep.tile([P, ROWS * DIM], BF16, name="w_raw%d" % c)
-            nc.sync.dma_start(
-                out=raw[:],
-                in_=W[c * CHUNK : (c + 1) * CHUNK, :].rearrange("(p r) d -> p (r d)", r=ROWS),
-            )
-            w_raw.append(raw)
+            rows = CHUNK // PIECES[c]
+            for piece in range(PIECES[c]):
+                first = c * CHUNK + piece * rows
+                raw = keep.tile([P, rows // P * DIM], BF16, name="w_raw%d" % first)
+                nc.sync.dma_start(
+                    out=raw[:], in_=W[first : first + rows, :].rearrange("(p r) d -> p (r d)", r=rows // P)
+                )
+                w_raw += [(raw, bank) for bank in range(rows // BANK)]
+                if first == 0:
+                    nc.sync.dma_start(out=x_raw[:], in_=x.rearrange("b n d -> (b n) d"))
 
+        warm = keep.tile([P, 1], F32)
+        nc.vector.memset(warm[:], 0.0)
+        nc.scalar.copy(out=warm[:], in_=warm[:])
         ident = keep.tile([P, P], F32)
         make_identity(nc, ident[:])
 
@@ -59,86 +64,99 @@ def tile_get_qkv_s_kernel(tc, x, W, out_0, out_1, out_2):
         x_scales = keep.tile([P, P], U8, align_bytes=64)
         w_codes = keep.tile([P, CHUNKS, CHUNK], U32, align_bytes=64)
         w_scales = keep.tile([P, CHUNKS, CHUNK], U8, align_bytes=64)
-
-        def multiply_chunk(c):
-            acc = psum_acc.tile([P, CHUNK], F32)
-            nc.tensor.matmul_mx(
-                out=acc[:],
-                lhsT=x_codes[:].bitcast(FP8X4),
-                lhsT_scale=x_scales[:],
-                rhs=w_codes[:, c, :].bitcast(FP8X4),
-                rhs_scale=w_scales[:, c, :],
-                start=True,
-                stop=True,
-            )
-            return acc
-
-        def transpose_x():
-            x_words = x_raw[:].bitcast(F32)
-            turned = psum_x.tile([P, HALVES, P], F32)
-            for half in range(HALVES):
-                nc.tensor.transpose(turned[:, half, :], x_words[:, half:WORDS:HALVES], ident[:])
-            grouped = stage.tile([P, P * PACK], BF16, name="x_grouped", align_bytes=64)
-            nc.scalar.copy(
-                out=grouped[:].bitcast(F32).rearrange("q (m h) -> q m h", h=HALVES),
-                in_=turned[:].rearrange("q h m -> q m h"),
-            )
-            return grouped
-
-        def transpose_chunk(c):
-            w_words = w_raw[c][:].bitcast(F32)
-            grouped = stage.tile([P, CHUNK * PACK], BF16, name="w_grouped", align_bytes=64)
-            grouped_words = grouped[:].bitcast(F32)
-            bank_words = BANK_ROWS * P * HALVES
-            for bank in range(ROWS // BANK_ROWS):
-                turned = psum_w.tile([P, BANK_ROWS, HALVES, P], F32)
-                for r in range(BANK_ROWS):
-                    for half in range(HALVES):
-                        first = (bank * BANK_ROWS + r) * WORDS
-                        nc.tensor.transpose(
-                            turned[:, r, half, :], w_words[:, first + half : first + WORDS : HALVES], ident[:]
-                        )
-                nc.scalar.copy(
-                    out=grouped_words[:, bank * bank_words : (bank + 1) * bank_words].rearrange(
-                        "q (r p h) -> q r p h", r=BANK_ROWS, h=HALVES
-                    ),
-                    in_=turned[:].rearrange("q r h p -> q r p h"),
-                )
-            return grouped
-
-        def store_chunk(c, acc):
-            result = keep.tile([P, CHUNK], F32, name="result%d" % c)
-            nc.vector.tensor_copy(
-                out=result[:].rearrange("m (p r) -> m p r", r=ROWS),
-                in_=acc[:].rearrange("m (r p) -> m p r", r=ROWS),
-            )
-            part = outs[c // CHUNKS_PER_PART]
-            head = (c % CHUNKS_PER_PART) * CHUNK_HEADS
-            for b in range(BATCH):
-                nc.sync.dma_start(
-                    out=part[b, head : head + CHUNK_HEADS, :, :].rearrange("h n d -> n h d"),
-                    in_=result[b:P:BATCH, :].rearrange("n (h d) -> n h d", d=DIM_HEAD),
-                )
-
-        x_grouped = transpose_x()
-        nc.vector.quantize_mx(out=x_codes[:].bitcast(FP8X4), scales=x_scales[:], in_=x_grouped[:])
-
         grouped = {}
         acc = {}
-        for step in range(CHUNKS + STORE_LAG):
-            if step < CHUNKS:
-                grouped[step] = transpose_chunk(step)
 
-            c = step - STORE_LAG
-            if c >= 0:
-                store_chunk(c, acc[c])
+        def prepare_x():
+            x_words = x_raw[:].bitcast(F32)
+            turned = psum_w.tile([P, HALVES, P], F32, name="turned")
+            for half in range(HALVES):
+                nc.tensor.transpose(turned[:, half, :], x_words[:, half:WORDS:HALVES], ident[:])
+            x_grouped = keep.tile([P, P * PACK], BF16, align_bytes=64)
+            nc.vector.tensor_copy(
+                out=x_grouped[:].bitcast(F32).rearrange("q (n b h) -> q n b h", b=BATCH, h=HALVES),
+                in_=turned[:].rearrange("q h (b n) -> q n b h", b=BATCH),
+            )
+            nc.vector.quantize_mx(out=x_codes[:].bitcast(FP8X4), scales=x_scales[:], in_=x_grouped[:])
 
-            c = step - QUANTISE_LAG
-            if 0 <= c < CHUNKS:
+        def transpose_bank(c, bank):
+            if bank == 0:
+                grouped[c] = stage.tile([P, CHUNK * PACK], BF16, name="w_grouped", align_bytes=64)
+            raw, place = w_raw[c * BANKS + bank]
+            w_words = raw[:].bitcast(F32)
+            bank_words = BANK * HALVES
+            turned = psum_w.tile([P, BANK_ROWS, HALVES, P], F32, name="turned")
+            for r in range(BANK_ROWS):
+                first = (place * BANK_ROWS + r) * WORDS
+                for half in range(HALVES):
+                    nc.tensor.transpose(
+                        turned[:, r, half, :], w_words[:, first + half : first + WORDS : HALVES], ident[:]
+                    )
+            nc.scalar.copy(
+                out=grouped[c][:].bitcast(F32)[:, bank * bank_words : (bank + 1) * bank_words].rearrange(
+                    "q (r p h) -> q r p h", r=BANK_ROWS, h=HALVES
+                ),
+                in_=turned[:].rearrange("q r h p -> q r p h"),
+            )
+
+        def columns(c, piece, pieces):
+            rows = CHUNK // pieces
+            return slice(piece * rows, (piece + 1) * rows)
+
+        def quantise(c):
+            pieces = PIECES[c] if c == LAST else 1
+            for piece in range(pieces):
+                cols = columns(c, piece, pieces)
                 nc.vector.quantize_mx(
-                    out=w_codes[:, c, :].bitcast(FP8X4), scales=w_scales[:, c, :], in_=grouped[c][:]
+                    out=w_codes[:, c, cols].bitcast(FP8X4),
+                    scales=w_scales[:, c, cols],
+                    in_=grouped[c][:, cols.start * PACK : cols.stop * PACK],
                 )
 
-            c = step - MULTIPLY_LAG
-            if 0 <= c < CHUNKS:
-                acc[c] = multiply_chunk(c)
+        def multiply(c):
+            pieces = PIECES[c] if c == LAST else 1
+            for piece in range(pieces):
+                cols = columns(c, piece, pieces)
+                acc[c, piece] = psum_acc.tile([P, CHUNK], F32, name="acc")
+                nc.tensor.matmul_mx(
+                    out=acc[c, piece][:, : CHUNK // pieces],
+                    lhsT=x_codes[:].bitcast(FP8X4),
+                    lhsT_scale=x_scales[:],
+                    rhs=w_codes[:, c, cols].bitcast(FP8X4),
+                    rhs_scale=w_scales[:, c, cols],
+                    start=True,
+                    stop=True,
+                )
+
+        def store(c):
+            pieces = PIECES[c] if c == LAST else 1
+            part = outs[c * CHUNK // PART_ROWS]
+            rows = CHUNK // pieces
+            inner = CHUNK // PIECES[c] // P
+            for piece in range(pieces):
+                result = keep.tile([P, rows], F32, name="result%d_%d" % (c, piece))
+                target = result[:].rearrange("m (k p r) -> m k p r", p=P, r=inner)
+                source = acc[c, piece][:, :rows].rearrange("m (k r p) -> m k p r", p=P, r=inner)
+                if c == LAST and piece == 0:
+                    nc.scalar.copy(out=target, in_=source)
+                else:
+                    nc.vector.tensor_copy(out=target, in_=source)
+                head = (c * CHUNK % PART_ROWS + piece * rows) // DIM_HEAD
+                for b in range(BATCH):
+                    nc.sync.dma_start(
+                        out=part[b, head : head + rows // DIM_HEAD, :, :].rearrange("h n d -> n h d"),
+                        in_=result[b:P:BATCH, :].rearrange("n (h d) -> n h d", d=DIM_HEAD),
+                    )
+
+        for step in range(CHUNKS + 3):
+            if step < CHUNKS:
+                transpose_bank(step, 0)
+                if step == 0:
+                    prepare_x()
+                transpose_bank(step, 1)
+            if step >= 3:
+                store(step - 3)
+            if 1 <= step <= CHUNKS:
+                quantise(step - 1)
+            if 2 <= step <= CHUNKS + 1:
+                multiply(step - 2)

@@ -18,13 +18,13 @@ WORDS = DIM // 2
 HALVES = WORDS // P
 BANK_ROWS = 2
 PART_ROWS = HEADS * DIM_HEAD
-CHUNK = 512
-CHUNKS = PARTS * PART_ROWS // CHUNK
 BANK = BANK_ROWS * P
-BANKS = CHUNK // BANK
 
-PIECES = [2, 1, 1, 1, 1, 2]
-LAST = CHUNKS - 1
+ROWS = [512,512,512,512,512,512]
+PIECES = [2,1,1,1,1,2]
+CHUNKS = len(ROWS)
+FIRST = [sum(ROWS[:c]) for c in range(CHUNKS)]
+ORDER = "T0,0 X T0,1 T1,0 Q0 T1,1 T2,0 Q1 T2,1 M0 O0,0,512,V T3,0 Q2 T3,1 M1 O1,0,512,V T4,0 Q3 T4,1 M2 O2,0,512,V M3 O3,0,512,S T5,0 Q4 T5,1,V Q5,0,256 Q5,256,512 M4 O4,0,512,S M5,0,256 M5,256,512 O5,0,256,S O5,256,512,V"
 
 FLOPS = 2 * BATCH * TOKENS * DIM * PARTS * PART_ROWS
 
@@ -35,25 +35,28 @@ def tile_get_qkv_s_kernel(tc, x, W, out_0, out_1, out_2):
 
     with ExitStack() as ctx:
         keep = ctx.enter_context(tc.tile_pool(name="keep", bufs=1))
-        stage = ctx.enter_context(tc.tile_pool(name="stage", bufs=3))
+        stage = ctx.enter_context(tc.tile_pool(name="stage", bufs=4))
         psum_w = ctx.enter_context(tc.psum_pool(name="psum_w", bufs=4))
         psum_acc = ctx.enter_context(tc.psum_pool(name="psum_acc", bufs=4))
         ctx.enter_context(tc.manual_schedule())
 
         x_raw = keep.tile([P, DIM], BF16)
-        w_raw = []
+        w_raw = {}
         for c in range(CHUNKS):
-            rows = CHUNK // PIECES[c]
+            rows = ROWS[c] // PIECES[c]
             for piece in range(PIECES[c]):
-                first = c * CHUNK + piece * rows
+                first = FIRST[c] + piece * rows
                 raw = keep.tile([P, rows // P * DIM], BF16, name="w_raw%d" % first)
                 nc.sync.dma_start(
                     out=raw[:], in_=W[first : first + rows, :].rearrange("(p r) d -> p (r d)", r=rows // P)
                 )
-                w_raw += [(raw, bank) for bank in range(rows // BANK)]
+                for bank in range(rows // BANK):
+                    w_raw[c, piece * (rows // BANK) + bank] = (raw, bank)
                 if first == 0:
                     nc.sync.dma_start(out=x_raw[:], in_=x.rearrange("b n d -> (b n) d"))
 
+        zeros = keep.tile([P, P], F32)
+        nc.vector.memset(zeros[:], 0.0)
         warm = keep.tile([P, 1], F32)
         nc.vector.memset(warm[:], 0.0)
         nc.scalar.copy(out=warm[:], in_=warm[:])
@@ -62,10 +65,11 @@ def tile_get_qkv_s_kernel(tc, x, W, out_0, out_1, out_2):
 
         x_codes = keep.tile([P, P], U32, align_bytes=64)
         x_scales = keep.tile([P, P], U8, align_bytes=64)
-        w_codes = keep.tile([P, CHUNKS, CHUNK], U32, align_bytes=64)
-        w_scales = keep.tile([P, CHUNKS, CHUNK], U8, align_bytes=64)
+        w_codes = keep.tile([P, PARTS * PART_ROWS], U32, align_bytes=64)
+        w_scales = keep.tile([P, PARTS * PART_ROWS], U8, align_bytes=64)
         grouped = {}
         acc = {}
+        res = {}
 
         def prepare_x():
             x_words = x_raw[:].bitcast(F32)
@@ -79,10 +83,10 @@ def tile_get_qkv_s_kernel(tc, x, W, out_0, out_1, out_2):
             )
             nc.vector.quantize_mx(out=x_codes[:].bitcast(FP8X4), scales=x_scales[:], in_=x_grouped[:])
 
-        def transpose_bank(c, bank):
+        def transpose_bank(c, bank, copy):
             if bank == 0:
-                grouped[c] = stage.tile([P, CHUNK * PACK], BF16, name="w_grouped", align_bytes=64)
-            raw, place = w_raw[c * BANKS + bank]
+                grouped[c] = stage.tile([P, 512 * PACK], BF16, name="w_grouped", align_bytes=64)
+            raw, place = w_raw[c, bank]
             w_words = raw[:].bitcast(F32)
             bank_words = BANK * HALVES
             turned = psum_w.tile([P, BANK_ROWS, HALVES, P], F32, name="turned")
@@ -92,71 +96,70 @@ def tile_get_qkv_s_kernel(tc, x, W, out_0, out_1, out_2):
                     nc.tensor.transpose(
                         turned[:, r, half, :], w_words[:, first + half : first + WORDS : HALVES], ident[:]
                     )
-            nc.scalar.copy(
+            copy(
                 out=grouped[c][:].bitcast(F32)[:, bank * bank_words : (bank + 1) * bank_words].rearrange(
                     "q (r p h) -> q r p h", r=BANK_ROWS, h=HALVES
                 ),
                 in_=turned[:].rearrange("q r h p -> q r p h"),
             )
 
-        def columns(c, piece, pieces):
-            rows = CHUNK // pieces
-            return slice(piece * rows, (piece + 1) * rows)
+        def quantise(c, lo, hi):
+            cols = slice(FIRST[c] + lo, FIRST[c] + hi)
+            nc.vector.quantize_mx(
+                out=w_codes[:, cols].bitcast(FP8X4), scales=w_scales[:, cols], in_=grouped[c][:, lo * PACK : hi * PACK]
+            )
 
-        def quantise(c):
-            pieces = PIECES[c] if c == LAST else 1
-            for piece in range(pieces):
-                cols = columns(c, piece, pieces)
-                nc.vector.quantize_mx(
-                    out=w_codes[:, c, cols].bitcast(FP8X4),
-                    scales=w_scales[:, c, cols],
-                    in_=grouped[c][:, cols.start * PACK : cols.stop * PACK],
+        def multiply(c, lo, hi):
+            cols = slice(FIRST[c] + lo, FIRST[c] + hi)
+            acc[c, lo] = psum_acc.tile([P, 512], F32, name="acc")
+            nc.tensor.matmul_mx(
+                out=acc[c, lo][:, : hi - lo],
+                lhsT=x_codes[:].bitcast(FP8X4),
+                lhsT_scale=x_scales[:],
+                rhs=w_codes[:, cols].bitcast(FP8X4),
+                rhs_scale=w_scales[:, cols],
+                start=True,
+                stop=True,
+            )
+
+        def leave(c, lo, hi, how):
+            rows = hi - lo
+            inner = ROWS[c] // PIECES[c] // P
+            result = keep.tile([P, rows], F32, name="result%d_%d" % (c, lo))
+            target = result[:].rearrange("m (k p r) -> m k p r", p=P, r=inner)
+            source = acc[c, lo][:, :rows].rearrange("m (k r p) -> m k p r", p=P, r=inner)
+            if how == "S":
+                nc.scalar.copy(out=target, in_=source)
+            elif how == "V":
+                nc.vector.tensor_copy(out=target, in_=source)
+            else:
+                mid = P // 2
+                for k in range(rows // (P * inner)):
+                    nc.scalar.copy(out=target[:, k, :mid, :], in_=source[:, k, :mid, :])
+                for k in range(rows // (P * inner)):
+                    nc.vector.tensor_copy(out=target[:, k, mid:, :], in_=source[:, k, mid:, :])
+            part = outs[FIRST[c] // PART_ROWS]
+            head = (FIRST[c] % PART_ROWS + lo) // DIM_HEAD
+            for b in range(BATCH):
+                nc.sync.dma_start(
+                    out=part[b, head : head + rows // DIM_HEAD, :, :].rearrange("h n d -> n h d"),
+                    in_=result[b:P:BATCH, :].rearrange("n (h d) -> n h d", d=DIM_HEAD),
                 )
 
-        def multiply(c):
-            pieces = PIECES[c] if c == LAST else 1
-            for piece in range(pieces):
-                cols = columns(c, piece, pieces)
-                acc[c, piece] = psum_acc.tile([P, CHUNK], F32, name="acc")
-                nc.tensor.matmul_mx(
-                    out=acc[c, piece][:, : CHUNK // pieces],
-                    lhsT=x_codes[:].bitcast(FP8X4),
-                    lhsT_scale=x_scales[:],
-                    rhs=w_codes[:, c, cols].bitcast(FP8X4),
-                    rhs_scale=w_scales[:, c, cols],
-                    start=True,
-                    stop=True,
-                )
-
-        def store(c):
-            pieces = PIECES[c] if c == LAST else 1
-            part = outs[c * CHUNK // PART_ROWS]
-            rows = CHUNK // pieces
-            inner = CHUNK // PIECES[c] // P
-            for piece in range(pieces):
-                result = keep.tile([P, rows], F32, name="result%d_%d" % (c, piece))
-                target = result[:].rearrange("m (k p r) -> m k p r", p=P, r=inner)
-                source = acc[c, piece][:, :rows].rearrange("m (k r p) -> m k p r", p=P, r=inner)
-                if c == LAST and piece == 0:
-                    nc.scalar.copy(out=target, in_=source)
-                else:
-                    nc.vector.tensor_copy(out=target, in_=source)
-                head = (c * CHUNK % PART_ROWS + piece * rows) // DIM_HEAD
-                for b in range(BATCH):
-                    nc.sync.dma_start(
-                        out=part[b, head : head + rows // DIM_HEAD, :, :].rearrange("h n d -> n h d"),
-                        in_=result[b:P:BATCH, :].rearrange("n (h d) -> n h d", d=DIM_HEAD),
-                    )
-
-        for step in range(CHUNKS + 3):
-            if step < CHUNKS:
-                transpose_bank(step, 0)
-                if step == 0:
-                    prepare_x()
-                transpose_bank(step, 1)
-            if step >= 3:
-                store(step - 3)
-            if 1 <= step <= CHUNKS:
-                quantise(step - 1)
-            if 2 <= step <= CHUNKS + 1:
-                multiply(step - 2)
+        for word in ORDER.split(" "):
+            kind = word[:1]
+            if kind == "X":
+                prepare_x()
+                continue
+            fields = word[1:].split(",")
+            c = int(fields[0])
+            if kind == "T":
+                transpose_bank(c, int(fields[1]), nc.vector.tensor_copy if len(fields) > 2 else nc.scalar.copy)
+                continue
+            lo, hi = (int(fields[1]), int(fields[2])) if len(fields) > 2 else (0, ROWS[c])
+            if kind == "Q":
+                quantise(c, lo, hi)
+            elif kind == "M":
+                multiply(c, lo, hi)
+            elif kind == "O":
+                leave(c, lo, hi, fields[-1] if fields[-1] in ("S", "V", "B") else "V")

from contextlib import ExitStack

import concourse.mybir as mybir
from concourse.masks import make_identity

BF16 = mybir.dt.bfloat16
F32 = mybir.dt.float32
U32 = mybir.dt.uint32
U8 = mybir.dt.uint8
FP8X4 = mybir.dt.float8_e4m3fn_x4

P = 128
PACK = 4
BATCH, TOKENS, DIM = 2, 64, 512
HEADS, DIM_HEAD = 16, 64
PARTS = 3
WORDS = DIM // 2
HALVES = WORDS // P
BANK_ROWS = 2
PART_ROWS = HEADS * DIM_HEAD
BANK = BANK_ROWS * P

ROWS = [512,512,512,512,512,512]
PIECES = [2,1,1,1,1,2]
CHUNKS = len(ROWS)
FIRST = [sum(ROWS[:c]) for c in range(CHUNKS)]
ORDER = "T0,0 X T0,1 T1,0 Q0 T1,1 T2,0 Q1 T2,1 M0 O0,0,512,V T3,0 Q2 T3,1 M1 O1,0,512,V T4,0 Q3 T4,1 M2 O2,0,512,V M3 O3,0,512,S T5,0 Q4 T5,1,V Q5,0,256 Q5,256,512 M4 O4,0,512,S M5,0,256 M5,256,512 O5,0,256,S O5,256,512,V"

FLOPS = 2 * BATCH * TOKENS * DIM * PARTS * PART_ROWS


def tile_get_qkv_s_kernel(tc, x, W, out_0, out_1, out_2):
    nc = tc.nc
    outs = [out_0, out_1, out_2]

    with ExitStack() as ctx:
        keep = ctx.enter_context(tc.tile_pool(name="keep", bufs=1))
        stage = ctx.enter_context(tc.tile_pool(name="stage", bufs=4))
        psum_w = ctx.enter_context(tc.psum_pool(name="psum_w", bufs=4))
        psum_acc = ctx.enter_context(tc.psum_pool(name="psum_acc", bufs=4))
        ctx.enter_context(tc.manual_schedule())

        x_raw = keep.tile([P, DIM], BF16)
        w_raw = {}
        for c in range(CHUNKS):
            rows = ROWS[c] // PIECES[c]
            for piece in range(PIECES[c]):
                first = FIRST[c] + piece * rows
                raw = keep.tile([P, rows // P * DIM], BF16, name="w_raw%d" % first)
                nc.sync.dma_start(
                    out=raw[:], in_=W[first : first + rows, :].rearrange("(p r) d -> p (r d)", r=rows // P)
                )
                for bank in range(rows // BANK):
                    w_raw[c, piece * (rows // BANK) + bank] = (raw, bank)
                if first == 0:
                    nc.sync.dma_start(out=x_raw[:], in_=x.rearrange("b n d -> (b n) d"))

        zeros = keep.tile([P, P], F32)
        nc.vector.memset(zeros[:], 0.0)
        warm = keep.tile([P, 1], F32)
        nc.vector.memset(warm[:], 0.0)
        nc.scalar.copy(out=warm[:], in_=warm[:])
        ident = keep.tile([P, P], F32)
        make_identity(nc, ident[:])

        x_codes = keep.tile([P, P], U32, align_bytes=64)
        x_scales = keep.tile([P, P], U8, align_bytes=64)
        w_codes = keep.tile([P, PARTS * PART_ROWS], U32, align_bytes=64)
        w_scales = keep.tile([P, PARTS * PART_ROWS], U8, align_bytes=64)
        grouped = {}
        acc = {}
        res = {}

        def prepare_x():
            x_words = x_raw[:].bitcast(F32)
            turned = psum_w.tile([P, HALVES, P], F32, name="turned")
            for half in range(HALVES):
                nc.tensor.transpose(turned[:, half, :], x_words[:, half:WORDS:HALVES], ident[:])
            x_grouped = keep.tile([P, P * PACK], BF16, align_bytes=64)
            nc.vector.tensor_copy(
                out=x_grouped[:].bitcast(F32).rearrange("q (n b h) -> q n b h", b=BATCH, h=HALVES),
                in_=turned[:].rearrange("q h (b n) -> q n b h", b=BATCH),
            )
            nc.vector.quantize_mx(out=x_codes[:].bitcast(FP8X4), scales=x_scales[:], in_=x_grouped[:])

        def transpose_bank(c, bank, copy):
            if bank == 0:
                grouped[c] = stage.tile([P, 512 * PACK], BF16, name="w_grouped", align_bytes=64)
            raw, place = w_raw[c, bank]
            w_words = raw[:].bitcast(F32)
            bank_words = BANK * HALVES
            turned = psum_w.tile([P, BANK_ROWS, HALVES, P], F32, name="turned")
            for r in range(BANK_ROWS):
                first = (place * BANK_ROWS + r) * WORDS
                for half in range(HALVES):
                    nc.tensor.transpose(
                        turned[:, r, half, :], w_words[:, first + half : first + WORDS : HALVES], ident[:]
                    )
            copy(
                out=grouped[c][:].bitcast(F32)[:, bank * bank_words : (bank + 1) * bank_words].rearrange(
                    "q (r p h) -> q r p h", r=BANK_ROWS, h=HALVES
                ),
                in_=turned[:].rearrange("q r h p -> q r p h"),
            )

        def quantise(c, lo, hi):
            cols = slice(FIRST[c] + lo, FIRST[c] + hi)
            nc.vector.quantize_mx(
                out=w_codes[:, cols].bitcast(FP8X4), scales=w_scales[:, cols], in_=grouped[c][:, lo * PACK : hi * PACK]
            )

        def multiply(c, lo, hi):
            cols = slice(FIRST[c] + lo, FIRST[c] + hi)
            acc[c, lo] = psum_acc.tile([P, 512], F32, name="acc")
            nc.tensor.matmul_mx(
                out=acc[c, lo][:, : hi - lo],
                lhsT=x_codes[:].bitcast(FP8X4),
                lhsT_scale=x_scales[:],
                rhs=w_codes[:, cols].bitcast(FP8X4),
                rhs_scale=w_scales[:, cols],
                start=True,
                stop=True,
            )

        def leave(c, lo, hi, how):
            rows = hi - lo
            inner = ROWS[c] // PIECES[c] // P
            result = keep.tile([P, rows], F32, name="result%d_%d" % (c, lo))
            target = result[:].rearrange("m (k p r) -> m k p r", p=P, r=inner)
            source = acc[c, lo][:, :rows].rearrange("m (k r p) -> m k p r", p=P, r=inner)
            if how == "S":
                nc.scalar.copy(out=target, in_=source)
            elif how == "V":
                nc.vector.tensor_copy(out=target, in_=source)
            else:
                mid = P // 2
                for k in range(rows // (P * inner)):
                    nc.scalar.copy(out=target[:, k, :mid, :], in_=source[:, k, :mid, :])
                for k in range(rows // (P * inner)):
                    nc.vector.tensor_copy(out=target[:, k, mid:, :], in_=source[:, k, mid:, :])
            part = outs[FIRST[c] // PART_ROWS]
            head = (FIRST[c] % PART_ROWS + lo) // DIM_HEAD
            for b in range(BATCH):
                nc.sync.dma_start(
                    out=part[b, head : head + rows // DIM_HEAD, :, :].rearrange("h n d -> n h d"),
                    in_=result[b:P:BATCH, :].rearrange("n (h d) -> n h d", d=DIM_HEAD),
                )

        for word in ORDER.split(" "):
            kind = word[:1]
            if kind == "X":
                prepare_x()
                continue
            fields = word[1:].split(",")
            c = int(fields[0])
            if kind == "T":
                transpose_bank(c, int(fields[1]), nc.vector.tensor_copy if len(fields) > 2 else nc.scalar.copy)
                continue
            lo, hi = (int(fields[1]), int(fields[2])) if len(fields) > 2 else (0, ROWS[c])
            if kind == "Q":
                quantise(c, lo, hi)
            elif kind == "M":
                multiply(c, lo, hi)
            elif kind == "O":
                leave(c, lo, hi, fields[-1] if fields[-1] in ("S", "V", "B") else "V")
